import numpy as np
import ml_dtypes

BF16 = ml_dtypes.bfloat16


def bf(x):
    return np.asarray(x, np.float32).astype(BF16)


def f32(x):
    return np.asarray(x, np.float32)


def f64(x):
    return np.asarray(x).astype(np.float64)


def striped(idx):
    return np.tile(idx.reshape(-1, 16).T, (8, 1))


S, D, M, N, K, R = 256, 128, 128, 256, 9, 8


def setup_inputs():
    return {"table": bf(np.random.standard_normal((D, S))), "w": bf(np.random.standard_normal((D, M)) / np.sqrt(K * D)), "rest": bf(np.random.standard_normal((R * D, N))), "w_rest": bf(np.random.standard_normal((R * D, M)) / np.sqrt(K * D)), "bias": f32(0.3 * np.random.standard_normal((M, K))), "offs": striped(np.random.permutation(S)[:N])}


def reference(table, w, rest, w_rest, bias, offs):
    idx = offs[:16].T.reshape(-1)
    acc = f64(w).T @ f64(table)[:, idx] + f64(w_rest).T @ f64(rest)
    return acc + f64(bias).sum(axis=1, keepdims=True)

@@ -1,0 +1,43 @@
+import concourse.mybir as mybir
+
+P = 128
+N = 256
+S = 256
+R = 8
+K = R + 1
+
+FLOPS = 2 * K * P * P * N
+
+BF16, F32, U16 = mybir.dt.bfloat16, mybir.dt.float32, mybir.dt.uint16
+
+
+def tile_scattervertical_kernel(tc, table, w, rest, w_rest, bias, offs, out):
+    nc = tc.nc
+    with (
+        tc.tile_pool(name="held", bufs=1) as held,
+        tc.psum_pool(name="psum", bufs=1) as psum,
+    ):
+        offsets = held.tile([P, N // 16], U16, name="offsets")
+        table_sb = held.tile([P, S], BF16, name="table_sb")
+        w_sb = held.tile([P, P], BF16, name="w_sb")
+        w_rest_sb = held.tile([P, R, P], BF16, name="w_rest_sb")
+        rest_sb = held.tile([P, R, N], BF16, name="rest_sb")
+        bias_sb = held.tile([P, K], F32, name="bias_sb")
+
+        nc.sync.dma_start(offsets[:], offs)
+        nc.sync.dma_start(table_sb[:], table)
+        nc.sync.dma_start(w_sb[:], w)
+        nc.sync.dma_start(w_rest_sb[:], w_rest.rearrange("(k p) m -> p k m", p=P))
+        nc.scalar.dma_start(rest_sb[:], rest.rearrange("(k p) n -> p k n", p=P))
+        nc.scalar.dma_start(bias_sb[:], bias)
+
+        acc = psum.tile([P, N], F32, name="acc")
+        nc.tensor.matmul(acc[:], w_sb[:], table_sb[:].indirect(offsets[:]), start=True, stop=False)
+        for k in range(R):
+            nc.tensor.matmul(acc[:], w_rest_sb[:, k, :], rest_sb[:, k, :], start=False, stop=(k == R - 1))
+
+        bias_sum = held.tile([P, 1], F32, name="bias_sum")
+        nc.vector.reduce_sum(bias_sum[:], bias_sb[:], axis=mybir.AxisListType.X)
+        out_sb = held.tile([P, N], F32, name="out_sb")
+        nc.vector.tensor_scalar(out_sb[:], acc[:], bias_sum[:, 0:1], None, mybir.AluOpType.add)
+        nc.sync.dma_start(out, out_sb[:])

@@ -5,6 +5,8 @@ N = 256
 S = 256
 R = 8
 K = R + 1
+C = 4
+G = R // C
 
 FLOPS = 2 * K * P * P * N
 
@@ -20,21 +22,26 @@ def tile_scattervertical_kernel(tc, table, w, rest, w_rest, bias, offs, out):
         offsets = held.tile([P, N // 16], U16, name="offsets")
         table_sb = held.tile([P, S], BF16, name="table_sb")
         w_sb = held.tile([P, P], BF16, name="w_sb")
-        w_rest_sb = held.tile([P, R, P], BF16, name="w_rest_sb")
-        rest_sb = held.tile([P, R, N], BF16, name="rest_sb")
         bias_sb = held.tile([P, K], F32, name="bias_sb")
-
         nc.sync.dma_start(offsets[:], offs)
         nc.sync.dma_start(table_sb[:], table)
         nc.sync.dma_start(w_sb[:], w)
-        nc.sync.dma_start(w_rest_sb[:], w_rest.rearrange("(k p) m -> p k m", p=P))
-        nc.scalar.dma_start(rest_sb[:], rest.rearrange("(k p) n -> p k n", p=P))
+
+        w_rest_pieces = w_rest.rearrange("(c p g) m -> c p g m", c=C, g=G)
+        rest_pieces = rest.rearrange("(c p g) n -> c p g n", c=C, g=G)
+        w_rest_sb = [held.tile([P, G, P], BF16, name=f"w_rest_sb{c}") for c in range(C)]
+        rest_sb = [held.tile([P, G, N], BF16, name=f"rest_sb{c}") for c in range(C)]
+        for c in range(C):
+            nc.sync.dma_start(w_rest_sb[c][:], w_rest_pieces[c])
+            nc.scalar.dma_start(rest_sb[c][:], rest_pieces[c])
         nc.scalar.dma_start(bias_sb[:], bias)
 
         acc = psum.tile([P, N], F32, name="acc")
         nc.tensor.matmul(acc[:], w_sb[:], table_sb[:].indirect(offsets[:]), start=True, stop=False)
-        for k in range(R):
-            nc.tensor.matmul(acc[:], w_rest_sb[:, k, :], rest_sb[:, k, :], start=False, stop=(k == R - 1))
+        for c in range(C):
+            for g in range(G):
+                last = c == C - 1 and g == G - 1
+                nc.tensor.matmul(acc[:], w_rest_sb[c][:, g, :], rest_sb[c][:, g, :], start=False, stop=last)
 
         bias_sum = held.tile([P, 1], F32, name="bias_sum")
         nc.vector.reduce_sum(bias_sum[:], bias_sb[:], axis=mybir.AxisListType.X)

@@ -5,8 +5,6 @@ N = 256
 S = 256
 R = 8
 K = R + 1
-C = 4
-G = R // C
 
 FLOPS = 2 * K * P * P * N
 
@@ -22,26 +20,21 @@ def tile_scattervertical_kernel(tc, table, w, rest, w_rest, bias, offs, out):
         offsets = held.tile([P, N // 16], U16, name="offsets")
         table_sb = held.tile([P, S], BF16, name="table_sb")
         w_sb = held.tile([P, P], BF16, name="w_sb")
+        w_rest_sb = held.tile([P, R, P], BF16, name="w_rest_sb")
+        rest_sb = held.tile([P, R, N], BF16, name="rest_sb")
         bias_sb = held.tile([P, K], F32, name="bias_sb")
+
         nc.sync.dma_start(offsets[:], offs)
         nc.sync.dma_start(table_sb[:], table)
         nc.sync.dma_start(w_sb[:], w)
-
-        w_rest_pieces = w_rest.rearrange("(c p g) m -> c p g m", c=C, g=G)
-        rest_pieces = rest.rearrange("(c p g) n -> c p g n", c=C, g=G)
-        w_rest_sb = [held.tile([P, G, P], BF16, name=f"w_rest_sb{c}") for c in range(C)]
-        rest_sb = [held.tile([P, G, N], BF16, name=f"rest_sb{c}") for c in range(C)]
-        for c in range(C):
-            nc.sync.dma_start(w_rest_sb[c][:], w_rest_pieces[c])
-            nc.scalar.dma_start(rest_sb[c][:], rest_pieces[c])
+        nc.sync.dma_start(w_rest_sb[:], w_rest.rearrange("(p k) m -> p k m", k=R))
+        nc.scalar.dma_start(rest_sb[:], rest.rearrange("(p k) n -> p k n", k=R))
         nc.scalar.dma_start(bias_sb[:], bias)
 
         acc = psum.tile([P, N], F32, name="acc")
         nc.tensor.matmul(acc[:], w_sb[:], table_sb[:].indirect(offsets[:]), start=True, stop=False)
-        for c in range(C):
-            for g in range(G):
-                last = c == C - 1 and g == G - 1
-                nc.tensor.matmul(acc[:], w_rest_sb[c][:, g, :], rest_sb[c][:, g, :], start=False, stop=last)
+        for k in range(R):
+            nc.tensor.matmul(acc[:], w_rest_sb[:, k, :], rest_sb[:, k, :], start=False, stop=(k == R - 1))
 
         bias_sum = held.tile([P, 1], F32, name="bias_sum")
         nc.vector.reduce_sum(bias_sum[:], bias_sb[:], axis=mybir.AxisListType.X)

@@ -5,6 +5,10 @@ N = 256
 S = 256
 R = 8
 K = R + 1
+C = 4
+G = R // C
+BANK = 512
+WARM = 6
 
 FLOPS = 2 * K * P * P * N
 
@@ -20,21 +24,32 @@ def tile_scattervertical_kernel(tc, table, w, rest, w_rest, bias, offs, out):
         offsets = held.tile([P, N // 16], U16, name="offsets")
         table_sb = held.tile([P, S], BF16, name="table_sb")
         w_sb = held.tile([P, P], BF16, name="w_sb")
-        w_rest_sb = held.tile([P, R, P], BF16, name="w_rest_sb")
-        rest_sb = held.tile([P, R, N], BF16, name="rest_sb")
         bias_sb = held.tile([P, K], F32, name="bias_sb")
-
         nc.sync.dma_start(offsets[:], offs)
         nc.sync.dma_start(table_sb[:], table)
         nc.sync.dma_start(w_sb[:], w)
-        nc.sync.dma_start(w_rest_sb[:], w_rest.rearrange("(p k) m -> p k m", k=R))
-        nc.scalar.dma_start(rest_sb[:], rest.rearrange("(p k) n -> p k n", k=R))
+
+        w_rest_pieces = w_rest.rearrange("(c p g) m -> c p g m", c=C, g=G)
+        rest_pieces = rest.rearrange("(c p g) n -> c p g n", c=C, g=G)
+        w_rest_sb = [held.tile([P, G, P], BF16, name=f"w_rest_sb{c}") for c in range(C)]
+        rest_sb = [held.tile([P, G, N], BF16, name=f"rest_sb{c}") for c in range(C)]
+        for c in range(C):
+            nc.sync.dma_start(w_rest_sb[c][:], w_rest_pieces[c])
+            nc.scalar.dma_start(rest_sb[c][:], rest_pieces[c])
         nc.scalar.dma_start(bias_sb[:], bias)
+
+        zeros = held.tile([P, BANK], BF16, name="zeros")
+        nc.vector.memset(zeros[:], 0.0)
+        unread = psum.tile([P, BANK], F32, name="unread")
+        for i in range(WARM):
+            nc.tensor.matmul(unread[:], zeros[:, 0:P], zeros[:], start=True, stop=True)
 
         acc = psum.tile([P, N], F32, name="acc")
         nc.tensor.matmul(acc[:], w_sb[:], table_sb[:].indirect(offsets[:]), start=True, stop=False)
-        for k in range(R):
-            nc.tensor.matmul(acc[:], w_rest_sb[:, k, :], rest_sb[:, k, :], start=False, stop=(k == R - 1))
+        for c in range(C):
+            for g in range(G):
+                last = c == C - 1 and g == G - 1
+                nc.tensor.matmul(acc[:], w_rest_sb[c][:, g, :], rest_sb[c][:, g, :], start=False, stop=last)
 
         bias_sum = held.tile([P, 1], F32, name="bias_sum")
         nc.vector.reduce_sum(bias_sum[:], bias_sb[:], axis=mybir.AxisListType.X)

@@ -7,8 +7,7 @@ R = 8
 K = R + 1
 C = 4
 G = R // C
-BANK = 512
-WARM = 6
+WARM = 16
 
 FLOPS = 2 * K * P * P * N
 
@@ -21,13 +20,19 @@ def tile_scattervertical_kernel(tc, table, w, rest, w_rest, bias, offs, out):
         tc.tile_pool(name="held", bufs=1) as held,
         tc.psum_pool(name="psum", bufs=1) as psum,
     ):
+        zeros = held.tile([P, 128], BF16, name="zeros")
+        nc.vector.memset(zeros[:], 0.0)
+        unread = psum.tile([P, 128], F32, name="unread")
+        for i in range(WARM):
+            nc.tensor.matmul(unread[:], zeros[:, 0:P], zeros[:], start=True, stop=True)
+
         offsets = held.tile([P, N // 16], U16, name="offsets")
         table_sb = held.tile([P, S], BF16, name="table_sb")
         w_sb = held.tile([P, P], BF16, name="w_sb")
         bias_sb = held.tile([P, K], F32, name="bias_sb")
         nc.sync.dma_start(offsets[:], offs)
-        nc.sync.dma_start(table_sb[:], table)
         nc.sync.dma_start(w_sb[:], w)
+        nc.scalar.dma_start(table_sb[:], table)
 
         w_rest_pieces = w_rest.rearrange("(c p g) m -> c p g m", c=C, g=G)
         rest_pieces = rest.rearrange("(c p g) n -> c p g n", c=C, g=G)
@@ -36,13 +41,7 @@ def tile_scattervertical_kernel(tc, table, w, rest, w_rest, bias, offs, out):
         for c in range(C):
             nc.sync.dma_start(w_rest_sb[c][:], w_rest_pieces[c])
             nc.scalar.dma_start(rest_sb[c][:], rest_pieces[c])
-        nc.scalar.dma_start(bias_sb[:], bias)
-
-        zeros = held.tile([P, BANK], BF16, name="zeros")
-        nc.vector.memset(zeros[:], 0.0)
-        unread = psum.tile([P, BANK], F32, name="unread")
-        for i in range(WARM):
-            nc.tensor.matmul(unread[:], zeros[:, 0:P], zeros[:], start=True, stop=True)
+        nc.gpsimd.dma_start(bias_sb[:], bias)
 
         acc = psum.tile([P, N], F32, name="acc")
         nc.tensor.matmul(acc[:], w_sb[:], table_sb[:].indirect(offsets[:]), start=True, stop=False)
@@ -53,6 +52,8 @@ def tile_scattervertical_kernel(tc, table, w, rest, w_rest, bias, offs, out):
 
         bias_sum = held.tile([P, 1], F32, name="bias_sum")
         nc.vector.reduce_sum(bias_sum[:], bias_sb[:], axis=mybir.AxisListType.X)
-        out_sb = held.tile([P, N], F32, name="out_sb")
-        nc.vector.tensor_scalar(out_sb[:], acc[:], bias_sum[:, 0:1], None, mybir.AluOpType.add)
-        nc.sync.dma_start(out, out_sb[:])
+        H = N // 2
+        for h, queue in enumerate((nc.sync, nc.scalar)):
+            out_sb = held.tile([P, H], F32, name=f"out_sb{h}")
+            nc.vector.tensor_scalar(out_sb[:], acc[:, h * H : (h + 1) * H], bias_sum[:, 0:1], None, mybir.AluOpType.add)
+            queue.dma_start(out[:, h * H : (h + 1) * H], out_sb[:])

@@ -7,7 +7,7 @@ R = 8
 K = R + 1
 C = 4
 G = R // C
-WARM = 16
+WARM = 28
 
 FLOPS = 2 * K * P * P * N
 

@@ -7,7 +7,8 @@ R = 8
 K = R + 1
 C = 4
 G = R // C
-WARM = 28
+BANK = 512
+WARM = 6
 
 FLOPS = 2 * K * P * P * N
 
@@ -20,12 +21,6 @@ def tile_scattervertical_kernel(tc, table, w, rest, w_rest, bias, offs, out):
         tc.tile_pool(name="held", bufs=1) as held,
         tc.psum_pool(name="psum", bufs=1) as psum,
     ):
-        zeros = held.tile([P, 128], BF16, name="zeros")
-        nc.vector.memset(zeros[:], 0.0)
-        unread = psum.tile([P, 128], F32, name="unread")
-        for i in range(WARM):
-            nc.tensor.matmul(unread[:], zeros[:, 0:P], zeros[:], start=True, stop=True)
-
         offsets = held.tile([P, N // 16], U16, name="offsets")
         table_sb = held.tile([P, S], BF16, name="table_sb")
         w_sb = held.tile([P, P], BF16, name="w_sb")
@@ -33,6 +28,7 @@ def tile_scattervertical_kernel(tc, table, w, rest, w_rest, bias, offs, out):
         nc.sync.dma_start(offsets[:], offs)
         nc.sync.dma_start(w_sb[:], w)
         nc.scalar.dma_start(table_sb[:], table)
+        nc.sync.dma_start(bias_sb[:], bias)
 
         w_rest_pieces = w_rest.rearrange("(c p g) m -> c p g m", c=C, g=G)
         rest_pieces = rest.rearrange("(c p g) n -> c p g n", c=C, g=G)
@@ -41,7 +37,12 @@ def tile_scattervertical_kernel(tc, table, w, rest, w_rest, bias, offs, out):
         for c in range(C):
             nc.sync.dma_start(w_rest_sb[c][:], w_rest_pieces[c])
             nc.scalar.dma_start(rest_sb[c][:], rest_pieces[c])
-        nc.gpsimd.dma_start(bias_sb[:], bias)
+
+        zeros = held.tile([P, BANK], BF16, name="zeros")
+        nc.vector.memset(zeros[:], 0.0)
+        unread = psum.tile([P, BANK], F32, name="unread")
+        for i in range(WARM):
+            nc.tensor.matmul(unread[:], zeros[:, 0:P], zeros[:], start=True, stop=True)
 
         acc = psum.tile([P, N], F32, name="acc")
         nc.tensor.matmul(acc[:], w_sb[:], table_sb[:].indirect(offsets[:]), start=True, stop=False)

@@ -5,8 +5,11 @@ N = 256
 S = 256
 R = 8
 K = R + 1
+H = N // 2
 C = 4
 G = R // C
+WC = 2
+WG = R // WC
 BANK = 512
 WARM = 6
 
@@ -30,13 +33,14 @@ def tile_scattervertical_kernel(tc, table, w, rest, w_rest, bias, offs, out):
         nc.scalar.dma_start(table_sb[:], table)
         nc.sync.dma_start(bias_sb[:], bias)
 
-        w_rest_pieces = w_rest.rearrange("(c p g) m -> c p g m", c=C, g=G)
-        rest_pieces = rest.rearrange("(c p g) n -> c p g n", c=C, g=G)
-        w_rest_sb = [held.tile([P, G, P], BF16, name=f"w_rest_sb{c}") for c in range(C)]
+        w_rest_rows = w_rest.rearrange("(p k) m -> p k m", k=R)
+        rest_rows = rest.rearrange("(p k) n -> p k n", k=R)
+        w_rest_sb = [held.tile([P, WG, P], BF16, name=f"w_rest_sb{c}") for c in range(WC)]
         rest_sb = [held.tile([P, G, N], BF16, name=f"rest_sb{c}") for c in range(C)]
+        for c in range(WC):
+            nc.sync.dma_start(w_rest_sb[c][:], w_rest_rows[:, c * WG : (c + 1) * WG, :])
         for c in range(C):
-            nc.sync.dma_start(w_rest_sb[c][:], w_rest_pieces[c])
-            nc.scalar.dma_start(rest_sb[c][:], rest_pieces[c])
+            nc.scalar.dma_start(rest_sb[c][:], rest_rows[:, c * G : (c + 1) * G, :])
 
         zeros = held.tile([P, BANK], BF16, name="zeros")
         nc.vector.memset(zeros[:], 0.0)
@@ -44,17 +48,25 @@ def tile_scattervertical_kernel(tc, table, w, rest, w_rest, bias, offs, out):
         for i in range(WARM):
             nc.tensor.matmul(unread[:], zeros[:, 0:P], zeros[:], start=True, stop=True)
 
-        acc = psum.tile([P, N], F32, name="acc")
-        nc.tensor.matmul(acc[:], w_sb[:], table_sb[:].indirect(offsets[:]), start=True, stop=False)
+        acc = [psum.tile([P, H], F32, name=f"acc{h}") for h in range(2)]
+        for h in range(2):
+            half_list = offsets[:, h * (H // 16) : (h + 1) * (H // 16)]
+            nc.tensor.matmul(acc[h][:], w_sb[:], table_sb[:].indirect(half_list), start=True, stop=False)
         for c in range(C):
-            for g in range(G):
-                last = c == C - 1 and g == G - 1
-                nc.tensor.matmul(acc[:], w_rest_sb[c][:, g, :], rest_sb[c][:, g, :], start=False, stop=last)
+            for h in range(2):
+                for g in range(G):
+                    k = c * G + g
+                    nc.tensor.matmul(
+                        acc[h][:],
+                        w_rest_sb[k // WG][:, k % WG, :],
+                        rest_sb[c][:, g, h * H : (h + 1) * H],
+                        start=False,
+                        stop=(k == R - 1),
+                    )
 
         bias_sum = held.tile([P, 1], F32, name="bias_sum")
         nc.vector.reduce_sum(bias_sum[:], bias_sb[:], axis=mybir.AxisListType.X)
-        H = N // 2
         for h, queue in enumerate((nc.sync, nc.scalar)):
             out_sb = held.tile([P, H], F32, name=f"out_sb{h}")
-            nc.vector.tensor_scalar(out_sb[:], acc[:, h * H : (h + 1) * H], bias_sum[:, 0:1], None, mybir.AluOpType.add)
+            nc.vector.tensor_scalar(out_sb[:], acc[h][:], bias_sum[:, 0:1], None, mybir.AluOpType.add)
             queue.dma_start(out[:, h * H : (h + 1) * H], out_sb[:])

@@ -11,6 +11,7 @@ G = R // C
 WC = 2
 WG = R // WC
 BANK = 512
+REPEAT = BANK // P
 WARM = 6
 
 FLOPS = 2 * K * P * P * N
@@ -42,11 +43,12 @@ def tile_scattervertical_kernel(tc, table, w, rest, w_rest, bias, offs, out):
         for c in range(C):
             nc.scalar.dma_start(rest_sb[c][:], rest_rows[:, c * G : (c + 1) * G, :])
 
-        zeros = held.tile([P, BANK], BF16, name="zeros")
+        zeros = held.tile([P, P], BF16, name="zeros")
         nc.vector.memset(zeros[:], 0.0)
-        unread = psum.tile([P, BANK], F32, name="unread")
+        zeros_wide = zeros[:].unsqueeze(1).to_broadcast([P, REPEAT, P])
+        unread = psum.tile([P, REPEAT, P], F32, name="unread")
         for i in range(WARM):
-            nc.tensor.matmul(unread[:], zeros[:, 0:P], zeros[:], start=True, stop=True)
+            nc.tensor.matmul(unread[:], zeros[:], zeros_wide, start=True, stop=True)
 
         acc = [psum.tile([P, H], F32, name=f"acc{h}") for h in range(2)]
         for h in range(2):

@@ -6,17 +6,16 @@ S = 256
 R = 8
 K = R + 1
 H = N // 2
-C = 4
-G = R // C
-WC = 2
-WG = R // WC
+PIECES = (2, 2, 2, 1, 1)
 BANK = 512
 REPEAT = BANK // P
-WARM = 6
+WARM = 4
 
 FLOPS = 2 * K * P * P * N
 
 BF16, F32, U16 = mybir.dt.bfloat16, mybir.dt.float32, mybir.dt.uint16
+
+assert sum(PIECES) == R
 
 
 def tile_scattervertical_kernel(tc, table, w, rest, w_rest, bias, offs, out):
@@ -31,17 +30,17 @@ def tile_scattervertical_kernel(tc, table, w, rest, w_rest, bias, offs, out):
         bias_sb = held.tile([P, K], F32, name="bias_sb")
         nc.sync.dma_start(offsets[:], offs)
         nc.sync.dma_start(w_sb[:], w)
-        nc.scalar.dma_start(table_sb[:], table)
-        nc.sync.dma_start(bias_sb[:], bias)
+        nc.sync.dma_start(table_sb[:], table)
 
         w_rest_rows = w_rest.rearrange("(p k) m -> p k m", k=R)
         rest_rows = rest.rearrange("(p k) n -> p k n", k=R)
-        w_rest_sb = [held.tile([P, WG, P], BF16, name=f"w_rest_sb{c}") for c in range(WC)]
-        rest_sb = [held.tile([P, G, N], BF16, name=f"rest_sb{c}") for c in range(C)]
-        for c in range(WC):
-            nc.sync.dma_start(w_rest_sb[c][:], w_rest_rows[:, c * WG : (c + 1) * WG, :])
-        for c in range(C):
-            nc.scalar.dma_start(rest_sb[c][:], rest_rows[:, c * G : (c + 1) * G, :])
+        w_rest_sb = held.tile([P, R, P], BF16, name="w_rest_sb")
+        nc.sync.dma_start(w_rest_sb[:], w_rest_rows)
+        rest_sb = [held.tile([P, rows, N], BF16, name=f"rest_sb{c}") for c, rows in enumerate(PIECES)]
+        first_row = [sum(PIECES[:c]) for c in range(len(PIECES))]
+        for c, rows in enumerate(PIECES):
+            nc.sync.dma_start(rest_sb[c][:], rest_rows[:, first_row[c] : first_row[c] + rows, :])
+        nc.sync.dma_start(bias_sb[:], bias)
 
         zeros = held.tile([P, P], BF16, name="zeros")
         nc.vector.memset(zeros[:], 0.0)
@@ -54,13 +53,13 @@ def tile_scattervertical_kernel(tc, table, w, rest, w_rest, bias, offs, out):
         for h in range(2):
             half_list = offsets[:, h * (H // 16) : (h + 1) * (H // 16)]
             nc.tensor.matmul(acc[h][:], w_sb[:], table_sb[:].indirect(half_list), start=True, stop=False)
-        for c in range(C):
+        for c, rows in enumerate(PIECES):
             for h in range(2):
-                for g in range(G):
-                    k = c * G + g
+                for g in range(rows):
+                    k = first_row[c] + g
                     nc.tensor.matmul(
                         acc[h][:],
-                        w_rest_sb[k // WG][:, k % WG, :],
+                        w_rest_sb[:, k, :],
                         rest_sb[c][:, g, h * H : (h + 1) * H],
                         start=False,
                         stop=(k == R - 1),

@@ -67,7 +67,7 @@ def tile_scattervertical_kernel(tc, table, w, rest, w_rest, bias, offs, out):
 
         bias_sum = held.tile([P, 1], F32, name="bias_sum")
         nc.vector.reduce_sum(bias_sum[:], bias_sb[:], axis=mybir.AxisListType.X)
-        for h, queue in enumerate((nc.sync, nc.scalar)):
+        for h in range(2):
             out_sb = held.tile([P, H], F32, name=f"out_sb{h}")
             nc.vector.tensor_scalar(out_sb[:], acc[h][:], bias_sum[:, 0:1], None, mybir.AluOpType.add)
-            queue.dma_start(out[:, h * H : (h + 1) * H], out_sb[:])
+            nc.sync.dma_start(out[:, h * H : (h + 1) * H], out_sb[:])

@@ -10,6 +10,7 @@ PIECES = (2, 2, 2, 1, 1)
 BANK = 512
 REPEAT = BANK // P
 WARM = 4
+ALIGN = 256
 
 FLOPS = 2 * K * P * P * N
 
@@ -25,8 +26,8 @@ def tile_scattervertical_kernel(tc, table, w, rest, w_rest, bias, offs, out):
         tc.psum_pool(name="psum", bufs=1) as psum,
     ):
         offsets = held.tile([P, N // 16], U16, name="offsets")
-        table_sb = held.tile([P, S], BF16, name="table_sb")
-        w_sb = held.tile([P, P], BF16, name="w_sb")
+        table_sb = held.tile([P, S], BF16, name="table_sb", align_bytes=ALIGN)
+        w_sb = held.tile([P, P], BF16, name="w_sb", align_bytes=ALIGN)
         bias_sb = held.tile([P, K], F32, name="bias_sb")
         nc.sync.dma_start(offsets[:], offs)
         nc.sync.dma_start(w_sb[:], w)
@@ -34,9 +35,11 @@ def tile_scattervertical_kernel(tc, table, w, rest, w_rest, bias, offs, out):
 
         w_rest_rows = w_rest.rearrange("(p k) m -> p k m", k=R)
         rest_rows = rest.rearrange("(p k) n -> p k n", k=R)
-        w_rest_sb = held.tile([P, R, P], BF16, name="w_rest_sb")
+        w_rest_sb = held.tile([P, R, P], BF16, name="w_rest_sb", align_bytes=ALIGN)
         nc.sync.dma_start(w_rest_sb[:], w_rest_rows)
-        rest_sb = [held.tile([P, rows, N], BF16, name=f"rest_sb{c}") for c, rows in enumerate(PIECES)]
+        rest_sb = [
+            held.tile([P, rows, N], BF16, name=f"rest_sb{c}", align_bytes=ALIGN) for c, rows in enumerate(PIECES)
+        ]
         first_row = [sum(PIECES[:c]) for c in range(len(PIECES))]
         for c, rows in enumerate(PIECES):
             nc.sync.dma_start(rest_sb[c][:], rest_rows[:, first_row[c] : first_row[c] + rows, :])
@@ -68,6 +71,6 @@ def tile_scattervertical_kernel(tc, table, w, rest, w_rest, bias, offs, out):
         bias_sum = held.tile([P, 1], F32, name="bias_sum")
         nc.vector.reduce_sum(bias_sum[:], bias_sb[:], axis=mybir.AxisListType.X)
         for h in range(2):
-            out_sb = held.tile([P, H], F32, name=f"out_sb{h}")
+            out_sb = held.tile([P, H], F32, name=f"out_sb{h}", align_bytes=ALIGN)
             nc.vector.tensor_scalar(out_sb[:], acc[h][:], bias_sum[:, 0:1], None, mybir.AluOpType.add)
             nc.sync.dma_start(out[:, h * H : (h + 1) * H], out_sb[:])

import concourse.mybir as mybir

P = 128
N = 256
S = 256
R = 8
K = R + 1
H = N // 2
PIECES = (2, 2, 2, 1, 1)
BANK = 512
REPEAT = BANK // P
WARM = 4
ALIGN = 256

FLOPS = 2 * K * P * P * N

BF16, F32, U16 = mybir.dt.bfloat16, mybir.dt.float32, mybir.dt.uint16

assert sum(PIECES) == R


def tile_scattervertical_kernel(tc, table, w, rest, w_rest, bias, offs, out):
    nc = tc.nc
    with (
        tc.tile_pool(name="held", bufs=1) as held,
        tc.psum_pool(name="psum", bufs=1) as psum,
    ):
        offsets = held.tile([P, N // 16], U16, name="offsets")
        table_sb = held.tile([P, S], BF16, name="table_sb", align_bytes=ALIGN)
        w_sb = held.tile([P, P], BF16, name="w_sb", align_bytes=ALIGN)
        bias_sb = held.tile([P, K], F32, name="bias_sb")
        nc.sync.dma_start(offsets[:], offs)
        nc.sync.dma_start(w_sb[:], w)
        nc.sync.dma_start(table_sb[:], table)

        w_rest_rows = w_rest.rearrange("(p k) m -> p k m", k=R)
        rest_rows = rest.rearrange("(p k) n -> p k n", k=R)
        w_rest_sb = held.tile([P, R, P], BF16, name="w_rest_sb", align_bytes=ALIGN)
        nc.sync.dma_start(w_rest_sb[:], w_rest_rows)
        rest_sb = [
            held.tile([P, rows, N], BF16, name=f"rest_sb{c}", align_bytes=ALIGN) for c, rows in enumerate(PIECES)
        ]
        first_row = [sum(PIECES[:c]) for c in range(len(PIECES))]
        for c, rows in enumerate(PIECES):
            nc.sync.dma_start(rest_sb[c][:], rest_rows[:, first_row[c] : first_row[c] + rows, :])
        nc.sync.dma_start(bias_sb[:], bias)

        zeros = held.tile([P, P], BF16, name="zeros")
        nc.vector.memset(zeros[:], 0.0)
        zeros_wide = zeros[:].unsqueeze(1).to_broadcast([P, REPEAT, P])
        unread = psum.tile([P, REPEAT, P], F32, name="unread")
        for i in range(WARM):
            nc.tensor.matmul(unread[:], zeros[:], zeros_wide, start=True, stop=True)

        acc = [psum.tile([P, H], F32, name=f"acc{h}") for h in range(2)]
        for h in range(2):
            half_list = offsets[:, h * (H // 16) : (h + 1) * (H // 16)]
            nc.tensor.matmul(acc[h][:], w_sb[:], table_sb[:].indirect(half_list), start=True, stop=False)
        for c, rows in enumerate(PIECES):
            for h in range(2):
                for g in range(rows):
                    k = first_row[c] + g
                    nc.tensor.matmul(
                        acc[h][:],
                        w_rest_sb[:, k, :],
                        rest_sb[c][:, g, h * H : (h + 1) * H],
                        start=False,
                        stop=(k == R - 1),
                    )

        bias_sum = held.tile([P, 1], F32, name="bias_sum")
        nc.vector.reduce_sum(bias_sum[:], bias_sb[:], axis=mybir.AxisListType.X)
        for h in range(2):
            out_sb = held.tile([P, H], F32, name=f"out_sb{h}", align_bytes=ALIGN)
            nc.vector.tensor_scalar(out_sb[:], acc[h][:], bias_sum[:, 0:1], None, mybir.AluOpType.add)
            nc.sync.dma_start(out[:, h * H : (h + 1) * H], out_sb[:])
